import numpy as np
import ml_dtypes


def mxq(x, axis, fmt="e4m3"):
    dtype, down = {"e4m3": (ml_dtypes.float8_e4m3fn, 7), "e5m2": (ml_dtypes.float8_e5m2, 14)}[fmt]
    v = np.moveaxis(np.asarray(x, np.float32).astype(ml_dtypes.bfloat16).astype(np.float64), axis, -1)
    blocks = v.reshape(v.shape[:-1] + (-1, 32))
    amax = np.abs(blocks).max(-1, keepdims=True)
    byte = np.maximum(np.where(amax > 0, np.frexp(amax)[1] - 1 + 127, 0) - down, 1)
    scale = np.exp2(byte - 127.0)
    codes = (blocks / scale).astype(np.float32).astype(dtype).astype(np.float64)
    return np.moveaxis((codes * scale).reshape(v.shape), -1, axis)


WIDE = False


def mx_kscale(k):
    if not WIDE:
        return np.ones(k)
    levels = np.array([10, -10, 5, -5, 0])
    if k % 512:
        return np.exp2(np.random.permutation(np.resize(levels, k // 32))).repeat(32)
    a = np.empty((k // 512, 16))
    for p in range(k // 512):
        a[p, :8] = np.random.permutation(np.resize(levels, 8))
        for g in range(8):
            far = levels[np.abs(levels - a[p, g]) >= 10]
            a[p, g + 8] = far[np.random.randint(len(far))]
    return np.exp2(a.ravel()).repeat(32)


BF16 = ml_dtypes.bfloat16


def bf(x):
    return np.asarray(x, np.float32).astype(BF16)


def f64(x):
    return np.asarray(x).astype(np.float64)


B, H, S, D = 1, 4, 1024, 128
SIGMA_HS = np.array([5.0, 10.0, 20.0, 40.0])


def gaussian_prior(n_heads, len_q, len_k):
    i = np.arange(len_q)[:, None]
    j = np.arange(len_k)[None, :]
    diff2 = f64(j - i) ** 2
    sig2 = 2.0 * SIGMA_HS[:n_heads, None, None] ** 2
    gm = np.exp(-diff2[None, :, :] / sig2)
    return np.where((i >= j)[None, :, :], gm, 0.0)


def setup_inputs():
    s = mx_kscale(S)
    Q = np.random.standard_normal((B, H, S, D))
    K = np.random.standard_normal((B, H, S, D))
    V = np.random.standard_normal((B, H, S, D)) * 0.125 * np.sqrt(S)
    Q[..., 0] = np.log(2.0) * np.sqrt(D)
    K[..., 0] += np.log2(s)
    V = V / s[:, None] * np.mean(s)
    return {"Q": bf(Q), "K": bf(K), "V": bf(V),
            "attn_mask": np.random.random((B, H, S, S)) < 0.25}


def reference(Q, K, V, attn_mask):
    scores = f64(Q) @ f64(K).transpose(0, 1, 3, 2) / np.sqrt(D)
    scores = scores + gaussian_prior(H, S, S)[None]
    scores = np.where(np.asarray(attn_mask), -1e9, scores)
    e = np.exp(scores - scores.max(-1, keepdims=True))
    return (mxq(e, 3, "e4m3") @ mxq(f64(V), 2, "e4m3")) / e.sum(-1, keepdims=True)

@@ -1,0 +1,331 @@
+import math
+
+import concourse.mybir as mybir
+from concourse.masks import make_identity
+
+F32 = mybir.dt.float32
+BF16 = mybir.dt.bfloat16
+I32 = mybir.dt.int32
+U32 = mybir.dt.uint32
+U8 = mybir.dt.uint8
+FP8X4 = mybir.dt.float8_e4m3fn_x4
+ALU = mybir.AluOpType
+ACT = mybir.ActivationFunctionType
+
+P = 128
+H = 4
+S = 1024
+D = 128
+NB = S // P
+NBLK = H * NB
+SIGMA = (5.0, 10.0, 20.0, 40.0)
+FLOPS = 2 * 2 * H * S * S * D
+
+SCALE = 1.0 / math.sqrt(D)
+MASKED = -1.0e9 * math.sqrt(D)
+CUT = 30.0
+MASK_BUFS = 10
+GROUPS = (4, 4, 4, 4, 4, 4, 4, 2, 1, 1)
+
+
+def prior_deltas(h):
+    keep = []
+    for delta in range(0, S, P):
+        low = delta - (P - 1)
+        if low <= 0 or low * low / (2.0 * SIGMA[h] ** 2) < CUT:
+            keep.append(delta)
+    return keep
+
+
+def tile_gpsdpattention_kernel(tc, Q, K, V, attn_mask, out):
+    nc = tc.nc
+
+    q_view = Q.rearrange("o h (b p) d -> p (o h b) d", p=P)
+    k_view = K.rearrange("o h (b p) d -> p (o h b) d", p=P)
+    q_long = Q.rearrange("o h (p r) d -> p (o h) r d", p=P)
+    k_long = K.rearrange("o h (p r) d -> p (o h) r d", p=P)
+    v_view = V.rearrange("o h (g p t) d -> p (o h g) (t d)", p=P, t=4)
+    m_view = attn_mask.bitcast(I32).rearrange("o h (ib p) w -> p (o h ib) w", p=P)
+    o_view = out.rearrange("o h (ib p) d -> p (o h ib) d", p=P)
+
+    with tc.tile_pool(name="const", bufs=1) as const, tc.tile_pool(name="work", bufs=3) as work, tc.tile_pool(
+        name="masks", bufs=MASK_BUFS
+    ) as mask_pool, tc.psum_pool(name="ps_s", bufs=2) as ps_s, tc.psum_pool(name="ps_t", bufs=2) as ps_t, tc.psum_pool(
+        name="ps_o", bufs=2
+    ) as ps_o, tc.manual_schedule():
+        state = {}
+        k_raw = [const.tile([P, NB, D], BF16, name="k_raw%d" % h) for h in range(H)]
+        q_raw = [const.tile([P, NB, D], BF16, name="q_raw%d" % h) for h in range(H)]
+        v_raw = [const.tile([P, 2, 4 * D], BF16, name="v_raw%d" % h) for h in range(H)]
+
+        def load_mask(n):
+            mk = mask_pool.tile([P, 2 * S], I32, name="mk", tag="mk")
+            if n == NBLK - 1:
+                nc.sync.dma_start(out=mk[:, :S], in_=m_view[:, n, :S])
+                nc.sync.dma_start(out=mk[:, S:], in_=m_view[:, n, S:])
+            else:
+                nc.sync.dma_start(out=mk[:], in_=m_view[:, n, :])
+            state[("mk", n)] = mk
+
+        def load_qk(h):
+            nc.sync.dma_start(out=k_raw[h][:], in_=k_long[:, h, :, :])
+            nc.sync.dma_start(out=q_raw[h][:], in_=q_long[:, h, :, :])
+            nc.sync.dma_start(out=v_raw[h][:], in_=v_view[:, 2 * h : 2 * h + 2, :])
+
+        nc.sync.dma_start(out=k_raw[0][:], in_=k_view[:, 0:NB, :])
+        nc.scalar.dma_start(out=q_raw[0][:], in_=q_view[:, 0:NB, :])
+        load_mask(0)
+        nc.sync.dma_start(out=v_raw[0][:], in_=v_view[:, 0:2, :])
+        for n in range(1, 3):
+            load_mask(n)
+        load_qk(1)
+        for n in range(3, MASK_BUFS):
+            load_mask(n)
+
+        ident_b = const.tile([P, P], BF16, name="ident_b")
+        make_identity(nc, ident_b[:])
+        width = max(prior_deltas(H - 1)) + P
+        dist = const.tile([P, width], F32, name="dist")
+        nc.gpsimd.iota(dist[:], pattern=[[1, width]], base=0, channel_multiplier=-1, allow_small_or_imprecise_dtypes=True)
+        ident_f = const.tile([P, P], F32, name="ident_f")
+        make_identity(nc, ident_f[:])
+        dist_p = const.tile([P, width], F32, name="dist_p")
+        nc.vector.scalar_tensor_tensor(out=dist_p[:], in0=dist[:], scalar=-1.0e4, in1=dist[:], op0=ALU.mult, op1=ALU.max)
+        dist_2 = const.tile([P, width], F32, name="dist_2")
+        nc.scalar.activation(out=dist_2[:], in_=dist_p[:], func=ACT.Square)
+        prior = [const.tile([P, max(prior_deltas(h)) + P], F32, name="prior%d" % h) for h in range(H)]
+
+        def make_prior(h):
+            w_h = max(prior_deltas(h)) + P
+            nc.scalar.activation(out=prior[h][:], in_=dist_2[:, :w_h], func=ACT.Exp, scale=-1.0 / (2.0 * SIGMA[h] ** 2))
+            if h == 0:
+                nc.vector.tensor_scalar(
+                    out=prior[h][:], in0=prior[h][:], scalar1=math.sqrt(D), scalar2=None, op0=ALU.mult
+                )
+            else:
+                nc.gpsimd.tensor_scalar(
+                    out=prior[h][:], in0=prior[h][:], scalar1=math.sqrt(D), scalar2=0.0, op0=ALU.mult, op1=ALU.add
+                )
+
+        neg_max = const.tile([P, NBLK], F32, name="neg_max")
+        row_sum = const.tile([P, NBLK], F32, name="row_sum")
+        row_inv = const.tile([P, NBLK], F32, name="row_inv")
+        raw_max = const.tile([P, NBLK], F32, name="raw_max")
+
+        v_grp = [const.tile([P, 2, D, 4], BF16, name="v_grp%d" % h, align_bytes=64) for h in range(H)]
+        v_code = [const.tile([P, 2 * D], U32, name="v_code%d" % h, align_bytes=64) for h in range(H)]
+        v_scale = [const.tile([P, 2 * D], U8, name="v_scale%d" % h, align_bytes=64) for h in range(H)]
+
+        def regroup_v(h):
+            for g in range(2):
+                nc.gpsimd.tensor_scalar(
+                    out=v_grp[h][:, g, :, :],
+                    in0=v_raw[h][:, g, :].rearrange("p (t d) -> p d t", t=4),
+                    scalar1=1.0,
+                    scalar2=0.0,
+                    op0=ALU.mult,
+                    op1=ALU.add,
+                )
+
+        def quantise_v(h):
+            nc.vector.quantize_mx(
+                out=v_code[h][:].bitcast(FP8X4),
+                scales=v_scale[h][:],
+                in_=v_grp[h][:].rearrange("p g d t -> p (g d t)"),
+            )
+
+        q_t = [const.tile([P, S], BF16, name="q_t%d" % h) for h in range(H)]
+        k_t = [const.tile([P, S], BF16, name="k_t%d" % h) for h in range(H)]
+
+        def flip_in(raw, dst, half, on_vector):
+            pin = ps_t.tile([P, 512], BF16, name="pin", tag="t")
+            for b in range(4):
+                nc.tensor.transpose(pin[:, b * P : (b + 1) * P], raw[:, 4 * half + b, :], ident_b[:])
+            if on_vector:
+                nc.vector.tensor_copy(out=dst[:, 512 * half : 512 * (half + 1)], in_=pin[:])
+            else:
+                nc.scalar.copy(out=dst[:, 512 * half : 512 * (half + 1)], in_=pin[:])
+
+        def flip_long(raw, dst):
+            pin = ps_t.tile([P, S], BF16, name="pin8", tag="t")
+            for r in range(NB):
+                nc.tensor.transpose(pin[:, r * P : (r + 1) * P], raw[:, r, :], ident_b[:])
+            nc.scalar.copy(
+                out=dst[:].rearrange("d (p r) -> d p r", r=NB),
+                in_=pin[:].rearrange("d (r p) -> d p r", r=NB),
+            )
+
+        def scores(n):
+            h, ib = divmod(n, NB)
+            banks = []
+            for pl in range(2):
+                ps = ps_s.tile([P, 512], F32, name="ps%d" % pl, tag="s%d" % pl)
+                adds = [b for b in range(4) if P * (ib - 4 * pl - b) in prior_deltas(h)]
+                nc.tensor.matmul(
+                    ps[:],
+                    lhsT=q_t[h][:, ib * P : (ib + 1) * P],
+                    rhs=k_t[h][:, pl * 512 : (pl + 1) * 512],
+                    start=True,
+                    stop=(len(adds) == 0),
+                )
+                for b in adds:
+                    x0 = P * (ib - 4 * pl - b)
+                    nc.tensor.matmul(
+                        ps[:, b * P : (b + 1) * P],
+                        lhsT=prior[h][:, x0 : x0 + P],
+                        rhs=ident_f[:],
+                        is_transpose=True,
+                        start=False,
+                        stop=(b == adds[-1]),
+                    )
+                banks.append(ps)
+            state[("ps", n)] = banks
+
+        def masked(n):
+            st = work.tile([P, S], F32, name="st", tag="st")
+            low_words = state[("mk", n)][:].rearrange("p (c f) -> p c f", f=2)
+            for pl in range(2):
+                nc.vector.scalar_tensor_tensor(
+                    out=st[:, pl * 512 : (pl + 1) * 512],
+                    in0=low_words[:, pl * 512 : (pl + 1) * 512, 0],
+                    scalar=MASKED,
+                    in1=state[("ps", n)][pl][:],
+                    op0=ALU.mult,
+                    op1=ALU.add,
+                )
+            state[("st", n)] = st
+
+        def row_max(n):
+            nc.vector.tensor_reduce(out=raw_max[:, n : n + 1], in_=state[("st", n)][:], axis=mybir.AxisListType.X, op=ALU.max)
+            nc.gpsimd.tensor_scalar(
+                out=neg_max[:, n : n + 1],
+                in0=raw_max[:, n : n + 1],
+                scalar1=-SCALE,
+                scalar2=0.0,
+                op0=ALU.mult,
+                op1=ALU.add,
+            )
+
+        def exps(n):
+            et = work.tile([P, S], BF16, name="et", tag="et")
+            nc.scalar.activation(
+                out=et[:],
+                in_=state[("st", n)][:],
+                func=ACT.Exp,
+                bias=neg_max[:, n : n + 1],
+                scale=SCALE,
+                accum_out=row_sum[:, n : n + 1],
+            )
+            state[("et", n)] = et
+
+        def flip(n):
+            pt = ps_t.tile([P, 4, P], F32, name="pt", tag="t")
+            words = state[("et", n)][:].bitcast(F32)
+            for g in range(2):
+                for u in range(2):
+                    nc.tensor.transpose(pt[:, 2 * g + u, :], words[:, 256 * g + u : 256 * (g + 1) : 2], ident_f[:])
+            state[("pt", n)] = pt
+
+        def regroup(n):
+            gt = work.tile([P, 2, P, 2], F32, name="gt", tag="gt", bufs=4, align_bytes=64)
+            nc.scalar.copy(out=gt[:], in_=state[("pt", n)][:].rearrange("p (g u) i -> p g i u", u=2))
+            state[("gt", n)] = gt
+
+        def quant(n):
+            cd = work.tile([P, 2 * P], U32, name="cd", tag="cd", align_bytes=64)
+            sc = work.tile([P, 2 * P], U8, name="sc", tag="sc", align_bytes=64)
+            nc.vector.quantize_mx(
+                out=cd[:].bitcast(FP8X4),
+                scales=sc[:],
+                in_=state[("gt", n)][:].rearrange("p g i u -> p (g i u)").bitcast(BF16),
+            )
+            state[("cd", n)] = (cd, sc)
+
+        group_of = {}
+        first = 0
+        for gi, size in enumerate(GROUPS):
+            for k in range(size):
+                group_of[first + k] = (gi, first, size, k)
+            first += size
+        finished = []
+
+        def weighted(n):
+            h = n // NB
+            gi, n0, size, k = group_of[n]
+            if k == 0:
+                state["po"] = ps_o.tile([P, 4, D], F32, name="po", tag="o")
+            po = state["po"]
+            cd, sc = state[("cd", n)]
+            for g in range(2):
+                nc.tensor.matmul_mx(
+                    out=po[:, k, :],
+                    lhsT=cd[:, g * P : (g + 1) * P].bitcast(FP8X4),
+                    lhsT_scale=sc[:, g * P : (g + 1) * P],
+                    rhs=v_code[h][:, g * D : (g + 1) * D].bitcast(FP8X4),
+                    rhs_scale=v_scale[h][:, g * D : (g + 1) * D],
+                    start=(g == 0),
+                    stop=(g == 1),
+                )
+
+        def finish(n):
+            gi, n0, size, k = group_of[n]
+            if k != size - 1:
+                return
+            po = state["po"]
+            nc.vector.reciprocal(out=row_inv[:, n0 : n0 + size], in_=row_sum[:, n0 : n0 + size])
+            ot = const.tile([P, size, D], F32, name="ot%d" % gi)
+            for j in range(size):
+                nc.scalar.activation(
+                    out=ot[:, j, :], in_=po[:, j, :], func=ACT.Copy, scale=row_inv[:, n0 + j : n0 + j + 1]
+                )
+            finished.append((n0, size, ot))
+
+        make_prior(0)
+        flip_in(k_raw[0], k_t[0], 0, True)
+        flip_in(q_raw[0], q_t[0], 0, False)
+        flip_in(k_raw[0], k_t[0], 1, True)
+        regroup_v(0)
+        scores(0)
+        flip_in(q_raw[0], q_t[0], 1, False)
+        stored = 0
+        for t in range(NBLK + 3):
+            if t + 1 < NBLK:
+                scores(t + 1)
+            if t < NBLK:
+                masked(t)
+                nxt = t + MASK_BUFS
+                if nxt < NBLK:
+                    if nxt % NB == NB - 4 and nxt // NB + 1 < H:
+                        load_qk(nxt // NB + 1)
+                    load_mask(nxt)
+            if 0 <= t - 1 < NBLK:
+                flip(t - 1)
+            if 0 <= t - 3:
+                quant(t - 3)
+                weighted(t - 3)
+            if t < NBLK:
+                row_max(t)
+                exps(t)
+            if 0 <= t - 1 < NBLK:
+                regroup(t - 1)
+            if 0 <= t - 3:
+                finish(t - 3)
+            if t == 0:
+                quantise_v(0)
+            if t + 1 < H:
+                make_prior(t + 1)
+            h_next = (t + 5) // NB
+            if 0 < h_next < H:
+                if (t + 5) % NB == 0:
+                    regroup_v(h_next)
+                if (t + 5) % NB == 2:
+                    quantise_v(h_next)
+            h_flip, piece = divmod(t + 5, NB)
+            if 0 < h_flip < H and piece == 0:
+                flip_long(k_raw[h_flip], k_t[h_flip])
+            if 0 < h_flip < H and piece == 2:
+                flip_long(q_raw[h_flip], q_t[h_flip])
+            if t + MASK_BUFS >= NBLK - 1:
+                for n0, size, ot in finished[stored:]:
+                    nc.sync.dma_start(out=o_view[:, n0 : n0 + size, :], in_=ot[:])
+                stored = len(finished)

@@ -40,8 +40,10 @@ def prior_deltas(h):
 def tile_gpsdpattention_kernel(tc, Q, K, V, attn_mask, out):
     nc = tc.nc
 
-    q_view = Q.rearrange("o h (b p) d -> p (o h b) d", p=P)
-    k_view = K.rearrange("o h (b p) d -> p (o h b) d", p=P)
+    q_flat = Q.rearrange("o h s d -> (o h s) d")
+    k_flat = K.rearrange("o h s d -> (o h s) d")
+    k_half = [k_flat[512 * x : 512 * (x + 1), :].rearrange("(p r) d -> p r d", r=4) for x in range(2)]
+    q_rest = q_flat[P:S, :].rearrange("(p r) d -> p r d", r=NB - 1)
     q_long = Q.rearrange("o h (p r) d -> p (o h) r d", p=P)
     k_long = K.rearrange("o h (p r) d -> p (o h) r d", p=P)
     v_view = V.rearrange("o h (g p t) d -> p (o h g) (t d)", p=P, t=4)
@@ -60,8 +62,11 @@ def tile_gpsdpattention_kernel(tc, Q, K, V, attn_mask, out):
 
         def load_mask(n):
             mk = mask_pool.tile([P, 2 * S], I32, name="mk", tag="mk")
-            if n == NBLK - 1:
+            if n in (0, NBLK - 1):
                 nc.sync.dma_start(out=mk[:, :S], in_=m_view[:, n, :S])
+                if n == 0:
+                    nc.sync.dma_start(out=k_raw[0][:, 4:, :], in_=k_half[1])
+                    nc.sync.dma_start(out=q_raw[0][:, 1:, :], in_=q_rest)
                 nc.sync.dma_start(out=mk[:, S:], in_=m_view[:, n, S:])
             else:
                 nc.sync.dma_start(out=mk[:], in_=m_view[:, n, :])
@@ -72,12 +77,12 @@ def tile_gpsdpattention_kernel(tc, Q, K, V, attn_mask, out):
             nc.sync.dma_start(out=q_raw[h][:], in_=q_long[:, h, :, :])
             nc.sync.dma_start(out=v_raw[h][:], in_=v_view[:, 2 * h : 2 * h + 2, :])
 
-        nc.sync.dma_start(out=k_raw[0][:], in_=k_view[:, 0:NB, :])
-        nc.scalar.dma_start(out=q_raw[0][:], in_=q_view[:, 0:NB, :])
+        nc.sync.dma_start(out=k_raw[0][:, :4, :], in_=k_half[0])
+        nc.scalar.dma_start(out=q_raw[0][:, 0, :], in_=q_flat[0:P, :])
         load_mask(0)
+        load_mask(1)
         nc.sync.dma_start(out=v_raw[0][:], in_=v_view[:, 0:2, :])
-        for n in range(1, 3):
-            load_mask(n)
+        load_mask(2)
         load_qk(1)
         for n in range(3, MASK_BUFS):
             load_mask(n)
@@ -85,27 +90,30 @@ def tile_gpsdpattention_kernel(tc, Q, K, V, attn_mask, out):
         ident_b = const.tile([P, P], BF16, name="ident_b")
         make_identity(nc, ident_b[:])
         width = max(prior_deltas(H - 1)) + P
+        near = max(prior_deltas(0)) + P
         dist = const.tile([P, width], F32, name="dist")
-        nc.gpsimd.iota(dist[:], pattern=[[1, width]], base=0, channel_multiplier=-1, allow_small_or_imprecise_dtypes=True)
+        nc.gpsimd.iota(dist[:, :near], pattern=[[1, near]], base=0, channel_multiplier=-1, allow_small_or_imprecise_dtypes=True)
         ident_f = const.tile([P, P], F32, name="ident_f")
         make_identity(nc, ident_f[:])
-        dist_p = const.tile([P, width], F32, name="dist_p")
-        nc.vector.scalar_tensor_tensor(out=dist_p[:], in0=dist[:], scalar=-1.0e4, in1=dist[:], op0=ALU.mult, op1=ALU.max)
+        nc.gpsimd.iota(
+            dist[:, near:], pattern=[[1, width - near]], base=near, channel_multiplier=-1, allow_small_or_imprecise_dtypes=True
+        )
+        nc.vector.scalar_tensor_tensor(
+            out=dist[:, :P], in0=dist[:, :P], scalar=-1.0e4, in1=dist[:, :P], op0=ALU.mult, op1=ALU.max
+        )
         dist_2 = const.tile([P, width], F32, name="dist_2")
-        nc.scalar.activation(out=dist_2[:], in_=dist_p[:], func=ACT.Square)
+        nc.scalar.activation(out=dist_2[:, :near], in_=dist[:, :near], func=ACT.Square)
         prior = [const.tile([P, max(prior_deltas(h)) + P], F32, name="prior%d" % h) for h in range(H)]
 
         def make_prior(h):
             w_h = max(prior_deltas(h)) + P
-            nc.scalar.activation(out=prior[h][:], in_=dist_2[:, :w_h], func=ACT.Exp, scale=-1.0 / (2.0 * SIGMA[h] ** 2))
-            if h == 0:
-                nc.vector.tensor_scalar(
-                    out=prior[h][:], in0=prior[h][:], scalar1=math.sqrt(D), scalar2=None, op0=ALU.mult
-                )
-            else:
-                nc.gpsimd.tensor_scalar(
-                    out=prior[h][:], in0=prior[h][:], scalar1=math.sqrt(D), scalar2=0.0, op0=ALU.mult, op1=ALU.add
-                )
+            nc.scalar.activation(
+                out=prior[h][:],
+                in_=dist_2[:, :w_h],
+                func=ACT.Exp,
+                scale=-1.0 / (2.0 * SIGMA[h] ** 2),
+                bias=0.5 * math.log(D),
+            )
 
         neg_max = const.tile([P, NBLK], F32, name="neg_max")
         row_sum = const.tile([P, NBLK], F32, name="row_sum")
@@ -116,8 +124,8 @@ def tile_gpsdpattention_kernel(tc, Q, K, V, attn_mask, out):
         v_code = [const.tile([P, 2 * D], U32, name="v_code%d" % h, align_bytes=64) for h in range(H)]
         v_scale = [const.tile([P, 2 * D], U8, name="v_scale%d" % h, align_bytes=64) for h in range(H)]
 
-        def regroup_v(h):
-            for g in range(2):
+        def regroup_v(h, passes):
+            for g in passes:
                 nc.gpsimd.tensor_scalar(
                     out=v_grp[h][:, g, :, :],
                     in0=v_raw[h][:, g, :].rearrange("p (t d) -> p d t", t=4),
@@ -137,28 +145,21 @@ def tile_gpsdpattention_kernel(tc, Q, K, V, attn_mask, out):
         q_t = [const.tile([P, S], BF16, name="q_t%d" % h) for h in range(H)]
         k_t = [const.tile([P, S], BF16, name="k_t%d" % h) for h in range(H)]
 
-        def flip_in(raw, dst, half, on_vector):
-            pin = ps_t.tile([P, 512], BF16, name="pin", tag="t")
-            for b in range(4):
-                nc.tensor.transpose(pin[:, b * P : (b + 1) * P], raw[:, 4 * half + b, :], ident_b[:])
+        def flip_in(raw, dst, r0, count, on_vector):
+            pin = ps_t.tile([P, count * P], BF16, name="pin", tag="t")
+            for r in range(count):
+                nc.tensor.transpose(pin[:, r * P : (r + 1) * P], raw[:, r0 + r, :], ident_b[:])
+            side = dst[:, r0 * P : (r0 + count) * P].rearrange("d (p r) -> d p r", r=count)
+            turned = pin[:].rearrange("d (r p) -> d p r", r=count)
             if on_vector:
-                nc.vector.tensor_copy(out=dst[:, 512 * half : 512 * (half + 1)], in_=pin[:])
+                nc.vector.tensor_copy(out=side, in_=turned)
             else:
-                nc.scalar.copy(out=dst[:, 512 * half : 512 * (half + 1)], in_=pin[:])
+                nc.scalar.copy(out=side, in_=turned)
 
-        def flip_long(raw, dst):
-            pin = ps_t.tile([P, S], BF16, name="pin8", tag="t")
-            for r in range(NB):
-                nc.tensor.transpose(pin[:, r * P : (r + 1) * P], raw[:, r, :], ident_b[:])
-            nc.scalar.copy(
-                out=dst[:].rearrange("d (p r) -> d p r", r=NB),
-                in_=pin[:].rearrange("d (r p) -> d p r", r=NB),
-            )
-
-        def scores(n):
+        def scores(n, halves=(0, 1)):
             h, ib = divmod(n, NB)
-            banks = []
-            for pl in range(2):
+            banks = state.setdefault(("ps", n), [])
+            for pl in halves:
                 ps = ps_s.tile([P, 512], F32, name="ps%d" % pl, tag="s%d" % pl)
                 adds = [b for b in range(4) if P * (ib - 4 * pl - b) in prior_deltas(h)]
                 nc.tensor.matmul(
@@ -179,7 +180,6 @@ def tile_gpsdpattention_kernel(tc, Q, K, V, attn_mask, out):
                         stop=(b == adds[-1]),
                     )
                 banks.append(ps)
-            state[("ps", n)] = banks
 
         def masked(n):
             st = work.tile([P, S], F32, name="st", tag="st")
@@ -281,12 +281,12 @@ def tile_gpsdpattention_kernel(tc, Q, K, V, attn_mask, out):
             finished.append((n0, size, ot))
 
         make_prior(0)
-        flip_in(k_raw[0], k_t[0], 0, True)
-        flip_in(q_raw[0], q_t[0], 0, False)
-        flip_in(k_raw[0], k_t[0], 1, True)
-        regroup_v(0)
-        scores(0)
-        flip_in(q_raw[0], q_t[0], 1, False)
+        flip_in(k_raw[0], k_t[0], 0, 4, True)
+        flip_in(q_raw[0], q_t[0], 0, 1, False)
+        scores(0, (0,))
+        flip_in(k_raw[0], k_t[0], 4, 4, False)
+        scores(0, (1,))
+        flip_in(q_raw[0], q_t[0], 1, NB - 1, False)
         stored = 0
         for t in range(NBLK + 3):
             if t + 1 < NBLK:
@@ -311,20 +311,24 @@ def tile_gpsdpattention_kernel(tc, Q, K, V, attn_mask, out):
             if 0 <= t - 3:
                 finish(t - 3)
             if t == 0:
-                quantise_v(0)
+                nc.scalar.activation(out=dist_2[:, near:], in_=dist[:, near:], func=ACT.Square)
             if t + 1 < H:
                 make_prior(t + 1)
+            if t < 2:
+                regroup_v(0, (t,))
+            if t == 2:
+                quantise_v(0)
             h_next = (t + 5) // NB
             if 0 < h_next < H:
                 if (t + 5) % NB == 0:
-                    regroup_v(h_next)
+                    regroup_v(h_next, (0, 1))
                 if (t + 5) % NB == 2:
                     quantise_v(h_next)
             h_flip, piece = divmod(t + 5, NB)
             if 0 < h_flip < H and piece == 0:
-                flip_long(k_raw[h_flip], k_t[h_flip])
+                flip_in(k_raw[h_flip], k_t[h_flip], 0, NB, False)
             if 0 < h_flip < H and piece == 2:
-                flip_long(q_raw[h_flip], q_t[h_flip])
+                flip_in(q_raw[h_flip], q_t[h_flip], 0, NB, False)
             if t + MASK_BUFS >= NBLK - 1:
                 for n0, size, ot in finished[stored:]:
                     nc.sync.dma_start(out=o_view[:, n0 : n0 + size, :], in_=ot[:])

@@ -209,8 +209,8 @@ def tile_gpsdpattention_kernel(tc, Q, K, V, attn_mask, out):
         def exps(n):
             et = work.tile([P, S], BF16, name="et", tag="et")
             nc.scalar.activation(
-                out=et[:],
-                in_=state[("st", n)][:],
+                out=et[:].rearrange("p (u x s) -> p u x s", u=2, s=2),
+                in_=state[("st", n)][:].rearrange("p (x u s) -> p u x s", u=2, s=2),
                 func=ACT.Exp,
                 bias=neg_max[:, n : n + 1],
                 scale=SCALE,
@@ -223,7 +223,7 @@ def tile_gpsdpattention_kernel(tc, Q, K, V, attn_mask, out):
             words = state[("et", n)][:].bitcast(F32)
             for g in range(2):
                 for u in range(2):
-                    nc.tensor.transpose(pt[:, 2 * g + u, :], words[:, 256 * g + u : 256 * (g + 1) : 2], ident_f[:])
+                    nc.tensor.transpose(pt[:, 2 * g + u, :], words[:, (2 * u + g) * P : (2 * u + g + 1) * P], ident_f[:])
             state[("pt", n)] = pt
 
         def regroup(n):

@@ -24,8 +24,11 @@ FLOPS = 2 * 2 * H * S * S * D
 SCALE = 1.0 / math.sqrt(D)
 MASKED = -1.0e9 * math.sqrt(D)
 CUT = 30.0
-MASK_BUFS = 10
-GROUPS = (4, 4, 4, 4, 4, 4, 4, 2, 1, 1)
+MASK_BUFS = 12
+BY_MATMUL = (12, 20, 28)
+EARLY = 2
+MASK_BF16 = -(2.0**34)
+GROUPS = (4, 4, 4, 4, 4, 4, 4, 3, 1)
 
 
 def prior_deltas(h):
@@ -66,26 +69,32 @@ def tile_gpsdpattention_kernel(tc, Q, K, V, attn_mask, out):
                 nc.sync.dma_start(out=mk[:, :S], in_=m_view[:, n, :S])
                 if n == 0:
                     nc.sync.dma_start(out=k_raw[0][:, 4:, :], in_=k_half[1])
-                    nc.sync.dma_start(out=q_raw[0][:, 1:, :], in_=q_rest)
                 nc.sync.dma_start(out=mk[:, S:], in_=m_view[:, n, S:])
+                if n == 0:
+                    nc.sync.dma_start(out=q_raw[0][:, 1:, :], in_=q_rest)
             else:
                 nc.sync.dma_start(out=mk[:], in_=m_view[:, n, :])
             state[("mk", n)] = mk
 
-        def load_qk(h):
-            nc.sync.dma_start(out=k_raw[h][:], in_=k_long[:, h, :, :])
-            nc.sync.dma_start(out=q_raw[h][:], in_=q_long[:, h, :, :])
-            nc.sync.dma_start(out=v_raw[h][:], in_=v_view[:, 2 * h : 2 * h + 2, :])
+        load_order = sorted(range(NBLK), key=lambda n: n - EARLY - 0.5 if n in BY_MATMUL else n)
+
+        def load_between(n):
+            h, ib = divmod(n + 4, NB)
+            if n == 1:
+                nc.sync.dma_start(out=v_raw[0][:], in_=v_view[:, 0:2, :])
+            if 0 < h < H:
+                if ib == 0:
+                    nc.sync.dma_start(out=k_raw[h][:], in_=k_long[:, h, :, :])
+                if ib == 1:
+                    nc.sync.dma_start(out=q_raw[h][:], in_=q_long[:, h, :, :])
+                if ib == 2:
+                    nc.sync.dma_start(out=v_raw[h][:], in_=v_view[:, 2 * h : 2 * h + 2, :])
 
         nc.sync.dma_start(out=k_raw[0][:, :4, :], in_=k_half[0])
         nc.scalar.dma_start(out=q_raw[0][:, 0, :], in_=q_flat[0:P, :])
-        load_mask(0)
-        load_mask(1)
-        nc.sync.dma_start(out=v_raw[0][:], in_=v_view[:, 0:2, :])
-        load_mask(2)
-        load_qk(1)
-        for n in range(3, MASK_BUFS):
-            load_mask(n)
+        for n in range(MASK_BUFS):
+            load_mask(load_order[n])
+            load_between(n)
 
         ident_b = const.tile([P, P], BF16, name="ident_b")
         make_identity(nc, ident_b[:])
@@ -119,6 +128,8 @@ def tile_gpsdpattention_kernel(tc, Q, K, V, attn_mask, out):
         row_sum = const.tile([P, NBLK], F32, name="row_sum")
         row_inv = const.tile([P, NBLK], F32, name="row_inv")
         raw_max = const.tile([P, NBLK], F32, name="raw_max")
+        half_max = const.tile([P, 2], F32, name="half_max")
+        half_sum = const.tile([P, 2], F32, name="half_sum")
 
         v_grp = [const.tile([P, 2, D, 4], BF16, name="v_grp%d" % h, align_bytes=64) for h in range(H)]
         v_code = [const.tile([P, 2 * D], U32, name="v_code%d" % h, align_bytes=64) for h in range(H)]
@@ -167,7 +178,7 @@ def tile_gpsdpattention_kernel(tc, Q, K, V, attn_mask, out):
                     lhsT=q_t[h][:, ib * P : (ib + 1) * P],
                     rhs=k_t[h][:, pl * 512 : (pl + 1) * 512],
                     start=True,
-                    stop=(len(adds) == 0),
+                    stop=(len(adds) == 0 and n not in BY_MATMUL),
                 )
                 for b in adds:
                     x0 = P * (ib - 4 * pl - b)
@@ -177,9 +188,30 @@ def tile_gpsdpattention_kernel(tc, Q, K, V, attn_mask, out):
                         rhs=ident_f[:],
                         is_transpose=True,
                         start=False,
-                        stop=(b == adds[-1]),
+                        stop=(b == adds[-1] and n not in BY_MATMUL),
                     )
                 banks.append(ps)
+
+        def mask_to_bf16(n, pl):
+            if pl == 0:
+                state[("mb", n)] = work.tile([P, S], BF16, name="mb", tag="mb", bufs=2)
+            low_words = state[("mk", n)][:].bitcast(U32).rearrange("p (c f) -> p c f", f=2)
+            nc.scalar.activation(
+                out=state[("mb", n)][:, pl * 512 : (pl + 1) * 512],
+                in_=low_words[:, pl * 512 : (pl + 1) * 512, 0],
+                func=ACT.Copy,
+                scale=MASK_BF16,
+            )
+
+        def mask_on_tensor(n):
+            for pl in range(2):
+                nc.tensor.matmul(
+                    state[("ps", n)][pl][:],
+                    lhsT=ident_b[:],
+                    rhs=state[("mb", n)][:, pl * 512 : (pl + 1) * 512],
+                    start=False,
+                    stop=True,
+                )
 
         def masked(n):
             st = work.tile([P, S], F32, name="st", tag="st")
@@ -218,28 +250,75 @@ def tile_gpsdpattention_kernel(tc, Q, K, V, attn_mask, out):
             )
             state[("et", n)] = et
 
-        def flip(n):
-            pt = ps_t.tile([P, 4, P], F32, name="pt", tag="t")
-            words = state[("et", n)][:].bitcast(F32)
+        def half_of_scores(n, g):
+            return state[("ps", n)][g][:] if n in BY_MATMUL else state[("st", n)][:, g * 512 : (g + 1) * 512]
+
+        def row_max_halves(n):
             for g in range(2):
-                for u in range(2):
-                    nc.tensor.transpose(pt[:, 2 * g + u, :], words[:, (2 * u + g) * P : (2 * u + g + 1) * P], ident_f[:])
-            state[("pt", n)] = pt
-
-        def regroup(n):
-            gt = work.tile([P, 2, P, 2], F32, name="gt", tag="gt", bufs=4, align_bytes=64)
-            nc.scalar.copy(out=gt[:], in_=state[("pt", n)][:].rearrange("p (g u) i -> p g i u", u=2))
-            state[("gt", n)] = gt
-
-        def quant(n):
-            cd = work.tile([P, 2 * P], U32, name="cd", tag="cd", align_bytes=64)
-            sc = work.tile([P, 2 * P], U8, name="sc", tag="sc", align_bytes=64)
-            nc.vector.quantize_mx(
-                out=cd[:].bitcast(FP8X4),
-                scales=sc[:],
-                in_=state[("gt", n)][:].rearrange("p g i u -> p (g i u)").bitcast(BF16),
+                nc.vector.tensor_reduce(
+                    out=half_max[:, g : g + 1], in_=half_of_scores(n, g), axis=mybir.AxisListType.X, op=ALU.max
+                )
+            nc.gpsimd.tensor_scalar(
+                out=neg_max[:, n : n + 1],
+                in0=half_max[:, 0:1],
+                scalar1=half_max[:, 1:2],
+                scalar2=-SCALE,
+                op0=ALU.max,
+                op1=ALU.mult,
             )
-            state[("cd", n)] = (cd, sc)
+
+        def exps_halves(n):
+            et = work.tile([P, S], BF16, name="et", tag="et")
+            for g in range(2):
+                nc.scalar.activation(
+                    out=et[:].rearrange("p (u g x s) -> p g u x s", u=2, g=2, s=2)[:, g, :, :, :],
+                    in_=half_of_scores(n, g).rearrange("p (x u s) -> p u x s", u=2, s=2),
+                    func=ACT.Exp,
+                    bias=neg_max[:, n : n + 1],
+                    scale=SCALE,
+                    accum_out=half_sum[:, g : g + 1],
+                )
+            nc.gpsimd.tensor_scalar(
+                out=row_sum[:, n : n + 1],
+                in0=half_sum[:, 0:1],
+                scalar1=half_sum[:, 1:2],
+                scalar2=0.0,
+                op0=ALU.add,
+                op1=ALU.add,
+            )
+            state[("et", n)] = et
+
+        def flip(n, passes=(0, 1)):
+            pt = ps_t.tile([P, 2 * len(passes), P], F32, name="pt", tag="t")
+            words = state[("et", n)][:].bitcast(F32)
+            for i, g in enumerate(passes):
+                for u in range(2):
+                    nc.tensor.transpose(pt[:, 2 * i + u, :], words[:, (2 * u + g) * P : (2 * u + g + 1) * P], ident_f[:])
+            state[("pt", n, passes)] = pt
+
+        def regroup(n, passes=(0, 1), on_vector=False):
+            if 0 in passes:
+                state[("gt", n)] = work.tile([P, 2, P, 2], F32, name="gt", tag="gt", bufs=4, align_bytes=64)
+            side = state[("gt", n)][:, passes[0] : passes[-1] + 1, :, :]
+            turned = state[("pt", n, passes)][:].rearrange("p (g u) i -> p g i u", u=2)
+            if on_vector:
+                nc.vector.tensor_copy(out=side, in_=turned)
+            else:
+                nc.scalar.copy(out=side, in_=turned)
+
+        def quant(n, passes=(0, 1)):
+            if 0 in passes:
+                state[("cd", n)] = (
+                    work.tile([P, 2 * P], U32, name="cd", tag="cd", align_bytes=64),
+                    work.tile([P, 2 * P], U8, name="sc", tag="sc", align_bytes=64),
+                )
+            cd, sc = state[("cd", n)]
+            cols = slice(passes[0] * P, (passes[-1] + 1) * P)
+            nc.vector.quantize_mx(
+                out=cd[:, cols].bitcast(FP8X4),
+                scales=sc[:, cols],
+                in_=state[("gt", n)][:, passes[0] : passes[-1] + 1, :, :].rearrange("p g i u -> p (g i u)").bitcast(BF16),
+            )
 
         group_of = {}
         first = 0
@@ -249,14 +328,14 @@ def tile_gpsdpattention_kernel(tc, Q, K, V, attn_mask, out):
             first += size
         finished = []
 
-        def weighted(n):
+        def weighted(n, passes=(0, 1)):
             h = n // NB
             gi, n0, size, k = group_of[n]
-            if k == 0:
+            if k == 0 and 0 in passes:
                 state["po"] = ps_o.tile([P, 4, D], F32, name="po", tag="o")
             po = state["po"]
             cd, sc = state[("cd", n)]
-            for g in range(2):
+            for g in passes:
                 nc.tensor.matmul_mx(
                     out=po[:, k, :],
                     lhsT=cd[:, g * P : (g + 1) * P].bitcast(FP8X4),
@@ -288,26 +367,29 @@ def tile_gpsdpattention_kernel(tc, Q, K, V, attn_mask, out):
         scores(0, (1,))
         flip_in(q_raw[0], q_t[0], 1, NB - 1, False)
         stored = 0
-        for t in range(NBLK + 3):
-            if t + 1 < NBLK:
-                scores(t + 1)
-            if t < NBLK:
+        for t in range(NBLK - 1):
+            scores(t + 1)
+            if t + 1 in BY_MATMUL:
+                mask_on_tensor(t + 1)
+            if t not in BY_MATMUL:
                 masked(t)
-                nxt = t + MASK_BUFS
-                if nxt < NBLK:
-                    if nxt % NB == NB - 4 and nxt // NB + 1 < H:
-                        load_qk(nxt // NB + 1)
-                    load_mask(nxt)
-            if 0 <= t - 1 < NBLK:
+            if t > 0:
                 flip(t - 1)
             if 0 <= t - 3:
                 quant(t - 3)
                 weighted(t - 3)
-            if t < NBLK:
+            if t in BY_MATMUL:
+                row_max_halves(t)
+                exps_halves(t)
+            else:
                 row_max(t)
                 exps(t)
-            if 0 <= t - 1 < NBLK:
+            if t > 0:
                 regroup(t - 1)
+            if t + 4 in BY_MATMUL:
+                mask_to_bf16(t + 4, 0)
+            if t + 3 in BY_MATMUL:
+                mask_to_bf16(t + 3, 1)
             if 0 <= t - 3:
                 finish(t - 3)
             if t == 0:
@@ -318,18 +400,46 @@ def tile_gpsdpattention_kernel(tc, Q, K, V, attn_mask, out):
                 regroup_v(0, (t,))
             if t == 2:
                 quantise_v(0)
-            h_next = (t + 5) // NB
-            if 0 < h_next < H:
-                if (t + 5) % NB == 0:
-                    regroup_v(h_next, (0, 1))
-                if (t + 5) % NB == 2:
-                    quantise_v(h_next)
-            h_flip, piece = divmod(t + 5, NB)
+            h_next, piece = divmod(t + 2, NB)
+            if 0 < h_next < H and piece == 0:
+                regroup_v(h_next, (0, 1))
+            if 0 < h_next < H and piece == 2:
+                quantise_v(h_next)
+            h_flip, piece = divmod(t + 4, NB)
             if 0 < h_flip < H and piece == 0:
                 flip_in(k_raw[h_flip], k_t[h_flip], 0, NB, False)
-            if 0 < h_flip < H and piece == 2:
+            if 0 < h_flip < H and piece == 1:
                 flip_in(q_raw[h_flip], q_t[h_flip], 0, NB, False)
+            if t + MASK_BUFS < NBLK:
+                load_mask(load_order[t + MASK_BUFS])
+                load_between(t + MASK_BUFS)
             if t + MASK_BUFS >= NBLK - 1:
                 for n0, size, ot in finished[stored:]:
                     nc.sync.dma_start(out=o_view[:, n0 : n0 + size, :], in_=ot[:])
                 stored = len(finished)
+
+        last = NBLK - 1
+        flip(last - 1)
+        masked(last)
+        quant(last - 3)
+        weighted(last - 3)
+        row_max(last)
+        quant(last - 2)
+        weighted(last - 2)
+        regroup(last - 1)
+        exps_halves(last)
+        quant(last - 1)
+        weighted(last - 1)
+        flip(last, (0,))
+        flip(last, (1,))
+        for n in range(last - 3, last):
+            finish(n)
+        regroup(last, (0,), on_vector=True)
+        regroup(last, (1,))
+        quant(last, (0,))
+        weighted(last, (0,))
+        quant(last, (1,))
+        weighted(last, (1,))
+        finish(last)
+        for n0, size, ot in finished[stored:]:
+            nc.sync.dma_start(out=o_view[:, n0 : n0 + size, :], in_=ot[:])

@@ -46,7 +46,7 @@ def tile_gpsdpattention_kernel(tc, Q, K, V, attn_mask, out):
     q_flat = Q.rearrange("o h s d -> (o h s) d")
     k_flat = K.rearrange("o h s d -> (o h s) d")
     k_half = [k_flat[512 * x : 512 * (x + 1), :].rearrange("(p r) d -> p r d", r=4) for x in range(2)]
-    q_rest = q_flat[P:S, :].rearrange("(p r) d -> p r d", r=NB - 1)
+    q_half = [q_flat[512 * x : 512 * (x + 1), :].rearrange("(p r) d -> p r d", r=4) for x in range(2)]
     q_long = Q.rearrange("o h (p r) d -> p (o h) r d", p=P)
     k_long = K.rearrange("o h (p r) d -> p (o h) r d", p=P)
     v_view = V.rearrange("o h (g p t) d -> p (o h g) (t d)", p=P, t=4)
@@ -67,11 +67,7 @@ def tile_gpsdpattention_kernel(tc, Q, K, V, attn_mask, out):
             mk = mask_pool.tile([P, 2 * S], I32, name="mk", tag="mk")
             if n in (0, NBLK - 1):
                 nc.sync.dma_start(out=mk[:, :S], in_=m_view[:, n, :S])
-                if n == 0:
-                    nc.sync.dma_start(out=k_raw[0][:, 4:, :], in_=k_half[1])
                 nc.sync.dma_start(out=mk[:, S:], in_=m_view[:, n, S:])
-                if n == 0:
-                    nc.sync.dma_start(out=q_raw[0][:, 1:, :], in_=q_rest)
             else:
                 nc.sync.dma_start(out=mk[:], in_=m_view[:, n, :])
             state[("mk", n)] = mk
@@ -81,6 +77,8 @@ def tile_gpsdpattention_kernel(tc, Q, K, V, attn_mask, out):
         def load_between(n):
             h, ib = divmod(n + 4, NB)
             if n == 1:
+                nc.sync.dma_start(out=q_raw[0][:, 4:, :], in_=q_half[1])
+            if n == 2:
                 nc.sync.dma_start(out=v_raw[0][:], in_=v_view[:, 0:2, :])
             if 0 < h < H:
                 if ib == 0:
@@ -91,7 +89,8 @@ def tile_gpsdpattention_kernel(tc, Q, K, V, attn_mask, out):
                     nc.sync.dma_start(out=v_raw[h][:], in_=v_view[:, 2 * h : 2 * h + 2, :])
 
         nc.sync.dma_start(out=k_raw[0][:, :4, :], in_=k_half[0])
-        nc.scalar.dma_start(out=q_raw[0][:, 0, :], in_=q_flat[0:P, :])
+        nc.sync.dma_start(out=q_raw[0][:, :4, :], in_=q_half[0])
+        nc.sync.dma_start(out=k_raw[0][:, 4:, :], in_=k_half[1])
         for n in range(MASK_BUFS):
             load_mask(load_order[n])
             load_between(n)
@@ -156,8 +155,8 @@ def tile_gpsdpattention_kernel(tc, Q, K, V, attn_mask, out):
         q_t = [const.tile([P, S], BF16, name="q_t%d" % h) for h in range(H)]
         k_t = [const.tile([P, S], BF16, name="k_t%d" % h) for h in range(H)]
 
-        def flip_in(raw, dst, r0, count, on_vector):
-            pin = ps_t.tile([P, count * P], BF16, name="pin", tag="t")
+        def flip_in(raw, dst, r0, count, on_vector=False, pool=ps_t, tag="t"):
+            pin = pool.tile([P, count * P], BF16, name="pin", tag=tag)
             for r in range(count):
                 nc.tensor.transpose(pin[:, r * P : (r + 1) * P], raw[:, r0 + r, :], ident_b[:])
             side = dst[:, r0 * P : (r0 + count) * P].rearrange("d (p r) -> d p r", r=count)
@@ -195,13 +194,16 @@ def tile_gpsdpattention_kernel(tc, Q, K, V, attn_mask, out):
         def mask_to_bf16(n, pl):
             if pl == 0:
                 state[("mb", n)] = work.tile([P, S], BF16, name="mb", tag="mb", bufs=2)
-            low_words = state[("mk", n)][:].bitcast(U32).rearrange("p (c f) -> p c f", f=2)
-            nc.scalar.activation(
-                out=state[("mb", n)][:, pl * 512 : (pl + 1) * 512],
-                in_=low_words[:, pl * 512 : (pl + 1) * 512, 0],
-                func=ACT.Copy,
-                scale=MASK_BF16,
-            )
+            low_halves = state[("mk", n)][:].bitcast(BF16).rearrange("p (c f) -> p c f", f=4)
+            for lo in (pl * 512, pl * 512 + 256):
+                nc.gpsimd.tensor_scalar(
+                    out=state[("mb", n)][:, lo : lo + 256],
+                    in0=low_halves[:, lo : lo + 256, 0],
+                    scalar1=2.0**127,
+                    scalar2=MASK_BF16 * 2.0**6,
+                    op0=ALU.mult,
+                    op1=ALU.mult,
+                )
 
         def mask_on_tensor(n):
             for pl in range(2):
@@ -360,12 +362,10 @@ def tile_gpsdpattention_kernel(tc, Q, K, V, attn_mask, out):
             finished.append((n0, size, ot))
 
         make_prior(0)
-        flip_in(k_raw[0], k_t[0], 0, 4, True)
-        flip_in(q_raw[0], q_t[0], 0, 1, False)
-        scores(0, (0,))
-        flip_in(k_raw[0], k_t[0], 4, 4, False)
-        scores(0, (1,))
-        flip_in(q_raw[0], q_t[0], 1, NB - 1, False)
+        flip_in(k_raw[0], k_t[0], 0, 4, on_vector=True)
+        flip_in(q_raw[0], q_t[0], 0, 4)
+        flip_in(k_raw[0], k_t[0], 4, 4, pool=ps_o, tag="o")
+        scores(0)
         stored = 0
         for t in range(NBLK - 1):
             scores(t + 1)
@@ -375,6 +375,8 @@ def tile_gpsdpattention_kernel(tc, Q, K, V, attn_mask, out):
                 masked(t)
             if t > 0:
                 flip(t - 1)
+            if t == 3:
+                quantise_v(0)
             if 0 <= t - 3:
                 quant(t - 3)
                 weighted(t - 3)
@@ -396,10 +398,10 @@ def tile_gpsdpattention_kernel(tc, Q, K, V, attn_mask, out):
                 nc.scalar.activation(out=dist_2[:, near:], in_=dist[:, near:], func=ACT.Square)
             if t + 1 < H:
                 make_prior(t + 1)
-            if t < 2:
-                regroup_v(0, (t,))
-            if t == 2:
-                quantise_v(0)
+            if t == 1:
+                flip_in(q_raw[0], q_t[0], 4, 4)
+            if t in (1, 2):
+                regroup_v(0, (t - 1,))
             h_next, piece = divmod(t + 2, NB)
             if 0 < h_next < H and piece == 0:
                 regroup_v(h_next, (0, 1))
@@ -407,9 +409,9 @@ def tile_gpsdpattention_kernel(tc, Q, K, V, attn_mask, out):
                 quantise_v(h_next)
             h_flip, piece = divmod(t + 4, NB)
             if 0 < h_flip < H and piece == 0:
-                flip_in(k_raw[h_flip], k_t[h_flip], 0, NB, False)
+                flip_in(k_raw[h_flip], k_t[h_flip], 0, NB)
             if 0 < h_flip < H and piece == 1:
-                flip_in(q_raw[h_flip], q_t[h_flip], 0, NB, False)
+                flip_in(q_raw[h_flip], q_t[h_flip], 0, NB)
             if t + MASK_BUFS < NBLK:
                 load_mask(load_order[t + MASK_BUFS])
                 load_between(t + MASK_BUFS)
@@ -421,21 +423,20 @@ def tile_gpsdpattention_kernel(tc, Q, K, V, attn_mask, out):
         last = NBLK - 1
         flip(last - 1)
         masked(last)
-        quant(last - 3)
-        weighted(last - 3)
-        row_max(last)
-        quant(last - 2)
-        weighted(last - 2)
-        regroup(last - 1)
+        row_max_halves(last)
+        for n in range(last - 3, last - 1):
+            quant(n)
+            weighted(n)
+        regroup(last - 1, on_vector=True)
         exps_halves(last)
         quant(last - 1)
-        weighted(last - 1)
         flip(last, (0,))
         flip(last, (1,))
-        for n in range(last - 3, last):
-            finish(n)
+        weighted(last - 1)
         regroup(last, (0,), on_vector=True)
         regroup(last, (1,))
+        for n in range(last - 3, last):
+            finish(n)
         quant(last, (0,))
         weighted(last, (0,))
         quant(last, (1,))

@@ -194,16 +194,13 @@ def tile_gpsdpattention_kernel(tc, Q, K, V, attn_mask, out):
         def mask_to_bf16(n, pl):
             if pl == 0:
                 state[("mb", n)] = work.tile([P, S], BF16, name="mb", tag="mb", bufs=2)
-            low_halves = state[("mk", n)][:].bitcast(BF16).rearrange("p (c f) -> p c f", f=4)
-            for lo in (pl * 512, pl * 512 + 256):
-                nc.gpsimd.tensor_scalar(
-                    out=state[("mb", n)][:, lo : lo + 256],
-                    in0=low_halves[:, lo : lo + 256, 0],
-                    scalar1=2.0**127,
-                    scalar2=MASK_BF16 * 2.0**6,
-                    op0=ALU.mult,
-                    op1=ALU.mult,
-                )
+            low_words = state[("mk", n)][:].bitcast(U32).rearrange("p (c f) -> p c f", f=2)
+            nc.scalar.activation(
+                out=state[("mb", n)][:, pl * 512 : (pl + 1) * 512],
+                in_=low_words[:, pl * 512 : (pl + 1) * 512, 0],
+                func=ACT.Copy,
+                scale=MASK_BF16,
+            )
 
         def mask_on_tensor(n):
             for pl in range(2):

import math

import concourse.mybir as mybir
from concourse.masks import make_identity

F32 = mybir.dt.float32
BF16 = mybir.dt.bfloat16
I32 = mybir.dt.int32
U32 = mybir.dt.uint32
U8 = mybir.dt.uint8
FP8X4 = mybir.dt.float8_e4m3fn_x4
ALU = mybir.AluOpType
ACT = mybir.ActivationFunctionType

P = 128
H = 4
S = 1024
D = 128
NB = S // P
NBLK = H * NB
SIGMA = (5.0, 10.0, 20.0, 40.0)
FLOPS = 2 * 2 * H * S * S * D

SCALE = 1.0 / math.sqrt(D)
MASKED = -1.0e9 * math.sqrt(D)
CUT = 30.0
MASK_BUFS = 12
BY_MATMUL = (12, 20, 28)
EARLY = 2
MASK_BF16 = -(2.0**34)
GROUPS = (4, 4, 4, 4, 4, 4, 4, 3, 1)


def prior_deltas(h):
    keep = []
    for delta in range(0, S, P):
        low = delta - (P - 1)
        if low <= 0 or low * low / (2.0 * SIGMA[h] ** 2) < CUT:
            keep.append(delta)
    return keep


def tile_gpsdpattention_kernel(tc, Q, K, V, attn_mask, out):
    nc = tc.nc

    q_flat = Q.rearrange("o h s d -> (o h s) d")
    k_flat = K.rearrange("o h s d -> (o h s) d")
    k_half = [k_flat[512 * x : 512 * (x + 1), :].rearrange("(p r) d -> p r d", r=4) for x in range(2)]
    q_half = [q_flat[512 * x : 512 * (x + 1), :].rearrange("(p r) d -> p r d", r=4) for x in range(2)]
    q_long = Q.rearrange("o h (p r) d -> p (o h) r d", p=P)
    k_long = K.rearrange("o h (p r) d -> p (o h) r d", p=P)
    v_view = V.rearrange("o h (g p t) d -> p (o h g) (t d)", p=P, t=4)
    m_view = attn_mask.bitcast(I32).rearrange("o h (ib p) w -> p (o h ib) w", p=P)
    o_view = out.rearrange("o h (ib p) d -> p (o h ib) d", p=P)

    with tc.tile_pool(name="const", bufs=1) as const, tc.tile_pool(name="work", bufs=3) as work, tc.tile_pool(
        name="masks", bufs=MASK_BUFS
    ) as mask_pool, tc.psum_pool(name="ps_s", bufs=2) as ps_s, tc.psum_pool(name="ps_t", bufs=2) as ps_t, tc.psum_pool(
        name="ps_o", bufs=2
    ) as ps_o, tc.manual_schedule():
        state = {}
        k_raw = [const.tile([P, NB, D], BF16, name="k_raw%d" % h) for h in range(H)]
        q_raw = [const.tile([P, NB, D], BF16, name="q_raw%d" % h) for h in range(H)]
        v_raw = [const.tile([P, 2, 4 * D], BF16, name="v_raw%d" % h) for h in range(H)]

        def load_mask(n):
            mk = mask_pool.tile([P, 2 * S], I32, name="mk", tag="mk")
            if n in (0, NBLK - 1):
                nc.sync.dma_start(out=mk[:, :S], in_=m_view[:, n, :S])
                nc.sync.dma_start(out=mk[:, S:], in_=m_view[:, n, S:])
            else:
                nc.sync.dma_start(out=mk[:], in_=m_view[:, n, :])
            state[("mk", n)] = mk

        load_order = sorted(range(NBLK), key=lambda n: n - EARLY - 0.5 if n in BY_MATMUL else n)

        def load_between(n):
            h, ib = divmod(n + 4, NB)
            if n == 1:
                nc.sync.dma_start(out=q_raw[0][:, 4:, :], in_=q_half[1])
            if n == 2:
                nc.sync.dma_start(out=v_raw[0][:], in_=v_view[:, 0:2, :])
            if 0 < h < H:
                if ib == 0:
                    nc.sync.dma_start(out=k_raw[h][:], in_=k_long[:, h, :, :])
                if ib == 1:
                    nc.sync.dma_start(out=q_raw[h][:], in_=q_long[:, h, :, :])
                if ib == 2:
                    nc.sync.dma_start(out=v_raw[h][:], in_=v_view[:, 2 * h : 2 * h + 2, :])

        nc.sync.dma_start(out=k_raw[0][:, :4, :], in_=k_half[0])
        nc.sync.dma_start(out=q_raw[0][:, :4, :], in_=q_half[0])
        nc.sync.dma_start(out=k_raw[0][:, 4:, :], in_=k_half[1])
        for n in range(MASK_BUFS):
            load_mask(load_order[n])
            load_between(n)

        ident_b = const.tile([P, P], BF16, name="ident_b")
        make_identity(nc, ident_b[:])
        width = max(prior_deltas(H - 1)) + P
        near = max(prior_deltas(0)) + P
        dist = const.tile([P, width], F32, name="dist")
        nc.gpsimd.iota(dist[:, :near], pattern=[[1, near]], base=0, channel_multiplier=-1, allow_small_or_imprecise_dtypes=True)
        ident_f = const.tile([P, P], F32, name="ident_f")
        make_identity(nc, ident_f[:])
        nc.gpsimd.iota(
            dist[:, near:], pattern=[[1, width - near]], base=near, channel_multiplier=-1, allow_small_or_imprecise_dtypes=True
        )
        nc.vector.scalar_tensor_tensor(
            out=dist[:, :P], in0=dist[:, :P], scalar=-1.0e4, in1=dist[:, :P], op0=ALU.mult, op1=ALU.max
        )
        dist_2 = const.tile([P, width], F32, name="dist_2")
        nc.scalar.activation(out=dist_2[:, :near], in_=dist[:, :near], func=ACT.Square)
        prior = [const.tile([P, max(prior_deltas(h)) + P], F32, name="prior%d" % h) for h in range(H)]

        def make_prior(h):
            w_h = max(prior_deltas(h)) + P
            nc.scalar.activation(
                out=prior[h][:],
                in_=dist_2[:, :w_h],
                func=ACT.Exp,
                scale=-1.0 / (2.0 * SIGMA[h] ** 2),
                bias=0.5 * math.log(D),
            )

        neg_max = const.tile([P, NBLK], F32, name="neg_max")
        row_sum = const.tile([P, NBLK], F32, name="row_sum")
        row_inv = const.tile([P, NBLK], F32, name="row_inv")
        raw_max = const.tile([P, NBLK], F32, name="raw_max")
        half_max = const.tile([P, 2], F32, name="half_max")
        half_sum = const.tile([P, 2], F32, name="half_sum")

        v_grp = [const.tile([P, 2, D, 4], BF16, name="v_grp%d" % h, align_bytes=64) for h in range(H)]
        v_code = [const.tile([P, 2 * D], U32, name="v_code%d" % h, align_bytes=64) for h in range(H)]
        v_scale = [const.tile([P, 2 * D], U8, name="v_scale%d" % h, align_bytes=64) for h in range(H)]

        def regroup_v(h, passes):
            for g in passes:
                nc.gpsimd.tensor_scalar(
                    out=v_grp[h][:, g, :, :],
                    in0=v_raw[h][:, g, :].rearrange("p (t d) -> p d t", t=4),
                    scalar1=1.0,
                    scalar2=0.0,
                    op0=ALU.mult,
                    op1=ALU.add,
                )

        def quantise_v(h):
            nc.vector.quantize_mx(
                out=v_code[h][:].bitcast(FP8X4),
                scales=v_scale[h][:],
                in_=v_grp[h][:].rearrange("p g d t -> p (g d t)"),
            )

        q_t = [const.tile([P, S], BF16, name="q_t%d" % h) for h in range(H)]
        k_t = [const.tile([P, S], BF16, name="k_t%d" % h) for h in range(H)]

        def flip_in(raw, dst, r0, count, on_vector=False, pool=ps_t, tag="t"):
            pin = pool.tile([P, count * P], BF16, name="pin", tag=tag)
            for r in range(count):
                nc.tensor.transpose(pin[:, r * P : (r + 1) * P], raw[:, r0 + r, :], ident_b[:])
            side = dst[:, r0 * P : (r0 + count) * P].rearrange("d (p r) -> d p r", r=count)
            turned = pin[:].rearrange("d (r p) -> d p r", r=count)
            if on_vector:
                nc.vector.tensor_copy(out=side, in_=turned)
            else:
                nc.scalar.copy(out=side, in_=turned)

        def scores(n, halves=(0, 1)):
            h, ib = divmod(n, NB)
            banks = state.setdefault(("ps", n), [])
            for pl in halves:
                ps = ps_s.tile([P, 512], F32, name="ps%d" % pl, tag="s%d" % pl)
                adds = [b for b in range(4) if P * (ib - 4 * pl - b) in prior_deltas(h)]
                nc.tensor.matmul(
                    ps[:],
                    lhsT=q_t[h][:, ib * P : (ib + 1) * P],
                    rhs=k_t[h][:, pl * 512 : (pl + 1) * 512],
                    start=True,
                    stop=(len(adds) == 0 and n not in BY_MATMUL),
                )
                for b in adds:
                    x0 = P * (ib - 4 * pl - b)
                    nc.tensor.matmul(
                        ps[:, b * P : (b + 1) * P],
                        lhsT=prior[h][:, x0 : x0 + P],
                        rhs=ident_f[:],
                        is_transpose=True,
                        start=False,
                        stop=(b == adds[-1] and n not in BY_MATMUL),
                    )
                banks.append(ps)

        def mask_to_bf16(n, pl):
            if pl == 0:
                state[("mb", n)] = work.tile([P, S], BF16, name="mb", tag="mb", bufs=2)
            low_words = state[("mk", n)][:].bitcast(U32).rearrange("p (c f) -> p c f", f=2)
            nc.scalar.activation(
                out=state[("mb", n)][:, pl * 512 : (pl + 1) * 512],
                in_=low_words[:, pl * 512 : (pl + 1) * 512, 0],
                func=ACT.Copy,
                scale=MASK_BF16,
            )

        def mask_on_tensor(n):
            for pl in range(2):
                nc.tensor.matmul(
                    state[("ps", n)][pl][:],
                    lhsT=ident_b[:],
                    rhs=state[("mb", n)][:, pl * 512 : (pl + 1) * 512],
                    start=False,
                    stop=True,
                )

        def masked(n):
            st = work.tile([P, S], F32, name="st", tag="st")
            low_words = state[("mk", n)][:].rearrange("p (c f) -> p c f", f=2)
            for pl in range(2):
                nc.vector.scalar_tensor_tensor(
                    out=st[:, pl * 512 : (pl + 1) * 512],
                    in0=low_words[:, pl * 512 : (pl + 1) * 512, 0],
                    scalar=MASKED,
                    in1=state[("ps", n)][pl][:],
                    op0=ALU.mult,
                    op1=ALU.add,
                )
            state[("st", n)] = st

        def row_max(n):
            nc.vector.tensor_reduce(out=raw_max[:, n : n + 1], in_=state[("st", n)][:], axis=mybir.AxisListType.X, op=ALU.max)
            nc.gpsimd.tensor_scalar(
                out=neg_max[:, n : n + 1],
                in0=raw_max[:, n : n + 1],
                scalar1=-SCALE,
                scalar2=0.0,
                op0=ALU.mult,
                op1=ALU.add,
            )

        def exps(n):
            et = work.tile([P, S], BF16, name="et", tag="et")
            nc.scalar.activation(
                out=et[:].rearrange("p (u x s) -> p u x s", u=2, s=2),
                in_=state[("st", n)][:].rearrange("p (x u s) -> p u x s", u=2, s=2),
                func=ACT.Exp,
                bias=neg_max[:, n : n + 1],
                scale=SCALE,
                accum_out=row_sum[:, n : n + 1],
            )
            state[("et", n)] = et

        def half_of_scores(n, g):
            return state[("ps", n)][g][:] if n in BY_MATMUL else state[("st", n)][:, g * 512 : (g + 1) * 512]

        def row_max_halves(n):
            for g in range(2):
                nc.vector.tensor_reduce(
                    out=half_max[:, g : g + 1], in_=half_of_scores(n, g), axis=mybir.AxisListType.X, op=ALU.max
                )
            nc.gpsimd.tensor_scalar(
                out=neg_max[:, n : n + 1],
                in0=half_max[:, 0:1],
                scalar1=half_max[:, 1:2],
                scalar2=-SCALE,
                op0=ALU.max,
                op1=ALU.mult,
            )

        def exps_halves(n):
            et = work.tile([P, S], BF16, name="et", tag="et")
            for g in range(2):
                nc.scalar.activation(
                    out=et[:].rearrange("p (u g x s) -> p g u x s", u=2, g=2, s=2)[:, g, :, :, :],
                    in_=half_of_scores(n, g).rearrange("p (x u s) -> p u x s", u=2, s=2),
                    func=ACT.Exp,
                    bias=neg_max[:, n : n + 1],
                    scale=SCALE,
                    accum_out=half_sum[:, g : g + 1],
                )
            nc.gpsimd.tensor_scalar(
                out=row_sum[:, n : n + 1],
                in0=half_sum[:, 0:1],
                scalar1=half_sum[:, 1:2],
                scalar2=0.0,
                op0=ALU.add,
                op1=ALU.add,
            )
            state[("et", n)] = et

        def flip(n, passes=(0, 1)):
            pt = ps_t.tile([P, 2 * len(passes), P], F32, name="pt", tag="t")
            words = state[("et", n)][:].bitcast(F32)
            for i, g in enumerate(passes):
                for u in range(2):
                    nc.tensor.transpose(pt[:, 2 * i + u, :], words[:, (2 * u + g) * P : (2 * u + g + 1) * P], ident_f[:])
            state[("pt", n, passes)] = pt

        def regroup(n, passes=(0, 1), on_vector=False):
            if 0 in passes:
                state[("gt", n)] = work.tile([P, 2, P, 2], F32, name="gt", tag="gt", bufs=4, align_bytes=64)
            side = state[("gt", n)][:, passes[0] : passes[-1] + 1, :, :]
            turned = state[("pt", n, passes)][:].rearrange("p (g u) i -> p g i u", u=2)
            if on_vector:
                nc.vector.tensor_copy(out=side, in_=turned)
            else:
                nc.scalar.copy(out=side, in_=turned)

        def quant(n, passes=(0, 1)):
            if 0 in passes:
                state[("cd", n)] = (
                    work.tile([P, 2 * P], U32, name="cd", tag="cd", align_bytes=64),
                    work.tile([P, 2 * P], U8, name="sc", tag="sc", align_bytes=64),
                )
            cd, sc = state[("cd", n)]
            cols = slice(passes[0] * P, (passes[-1] + 1) * P)
            nc.vector.quantize_mx(
                out=cd[:, cols].bitcast(FP8X4),
                scales=sc[:, cols],
                in_=state[("gt", n)][:, passes[0] : passes[-1] + 1, :, :].rearrange("p g i u -> p (g i u)").bitcast(BF16),
            )

        group_of = {}
        first = 0
        for gi, size in enumerate(GROUPS):
            for k in range(size):
                group_of[first + k] = (gi, first, size, k)
            first += size
        finished = []

        def weighted(n, passes=(0, 1)):
            h = n // NB
            gi, n0, size, k = group_of[n]
            if k == 0 and 0 in passes:
                state["po"] = ps_o.tile([P, 4, D], F32, name="po", tag="o")
            po = state["po"]
            cd, sc = state[("cd", n)]
            for g in passes:
                nc.tensor.matmul_mx(
                    out=po[:, k, :],
                    lhsT=cd[:, g * P : (g + 1) * P].bitcast(FP8X4),
                    lhsT_scale=sc[:, g * P : (g + 1) * P],
                    rhs=v_code[h][:, g * D : (g + 1) * D].bitcast(FP8X4),
                    rhs_scale=v_scale[h][:, g * D : (g + 1) * D],
                    start=(g == 0),
                    stop=(g == 1),
                )

        def finish(n):
            gi, n0, size, k = group_of[n]
            if k != size - 1:
                return
            po = state["po"]
            nc.vector.reciprocal(out=row_inv[:, n0 : n0 + size], in_=row_sum[:, n0 : n0 + size])
            ot = const.tile([P, size, D], F32, name="ot%d" % gi)
            for j in range(size):
                nc.scalar.activation(
                    out=ot[:, j, :], in_=po[:, j, :], func=ACT.Copy, scale=row_inv[:, n0 + j : n0 + j + 1]
                )
            finished.append((n0, size, ot))

        make_prior(0)
        flip_in(k_raw[0], k_t[0], 0, 4, on_vector=True)
        flip_in(q_raw[0], q_t[0], 0, 4)
        flip_in(k_raw[0], k_t[0], 4, 4, pool=ps_o, tag="o")
        scores(0)
        stored = 0
        for t in range(NBLK - 1):
            scores(t + 1)
            if t + 1 in BY_MATMUL:
                mask_on_tensor(t + 1)
            if t not in BY_MATMUL:
                masked(t)
            if t > 0:
                flip(t - 1)
            if t == 3:
                quantise_v(0)
            if 0 <= t - 3:
                quant(t - 3)
                weighted(t - 3)
            if t in BY_MATMUL:
                row_max_halves(t)
                exps_halves(t)
            else:
                row_max(t)
                exps(t)
            if t > 0:
                regroup(t - 1)
            if t + 4 in BY_MATMUL:
                mask_to_bf16(t + 4, 0)
            if t + 3 in BY_MATMUL:
                mask_to_bf16(t + 3, 1)
            if 0 <= t - 3:
                finish(t - 3)
            if t == 0:
                nc.scalar.activation(out=dist_2[:, near:], in_=dist[:, near:], func=ACT.Square)
            if t + 1 < H:
                make_prior(t + 1)
            if t == 1:
                flip_in(q_raw[0], q_t[0], 4, 4)
            if t in (1, 2):
                regroup_v(0, (t - 1,))
            h_next, piece = divmod(t + 2, NB)
            if 0 < h_next < H and piece == 0:
                regroup_v(h_next, (0, 1))
            if 0 < h_next < H and piece == 2:
                quantise_v(h_next)
            h_flip, piece = divmod(t + 4, NB)
            if 0 < h_flip < H and piece == 0:
                flip_in(k_raw[h_flip], k_t[h_flip], 0, NB)
            if 0 < h_flip < H and piece == 1:
                flip_in(q_raw[h_flip], q_t[h_flip], 0, NB)
            if t + MASK_BUFS < NBLK:
                load_mask(load_order[t + MASK_BUFS])
                load_between(t + MASK_BUFS)
            if t + MASK_BUFS >= NBLK - 1:
                for n0, size, ot in finished[stored:]:
                    nc.sync.dma_start(out=o_view[:, n0 : n0 + size, :], in_=ot[:])
                stored = len(finished)

        last = NBLK - 1
        flip(last - 1)
        masked(last)
        row_max_halves(last)
        for n in range(last - 3, last - 1):
            quant(n)
            weighted(n)
        regroup(last - 1, on_vector=True)
        exps_halves(last)
        quant(last - 1)
        flip(last, (0,))
        flip(last, (1,))
        weighted(last - 1)
        regroup(last, (0,), on_vector=True)
        regroup(last, (1,))
        for n in range(last - 3, last):
            finish(n)
        quant(last, (0,))
        weighted(last, (0,))
        quant(last, (1,))
        weighted(last, (1,))
        finish(last)
        for n0, size, ot in finished[stored:]:
            nc.sync.dma_start(out=o_view[:, n0 : n0 + size, :], in_=ot[:])
